import numpy as np
import ml_dtypes

BF16 = ml_dtypes.bfloat16


def bf(x):
    return np.asarray(x, np.float32).astype(BF16)


def f32(x):
    return np.asarray(x, np.float32)


def f64(x):
    return np.asarray(x).astype(np.float64)


def striped(idx):
    return np.tile(idx.reshape(-1, 16).T, (8, 1))


D, H, S, N = 128, 4, 512, 512


def setup_inputs():
    return {
        "r_emb": f32(np.random.standard_normal((D, S))),
        "q": bf(0.3 * np.random.standard_normal((H * D, N))),
        "k": bf(0.4 * np.random.standard_normal((H * D, N))),
        "v": bf(np.random.standard_normal((N, H * D))),
        "r_bias": bf(np.random.standard_normal((H * D, 1)) / np.sqrt(D)),
        "attn_bias": f32(np.random.standard_normal((N, N))),
        "offs": striped(np.random.permutation(np.tile(np.arange(S), 2))[:N]),
    }


def reference(r_emb, q, k, v, r_bias, attn_bias, offs):
    idx = offs[:16].T.reshape(-1)
    rre = f64(r_emb)[:, idx]
    qh = f64(q).reshape(H, D, N)
    kh = f64(k).reshape(H, D, N)
    vh = f64(v).reshape(N, H, D)
    rb = f64(r_bias).reshape(H, D, 1)
    qr = (qh * rb).sum(axis=1, keepdims=True)
    q2 = rre[None] * qr + qh
    sc = np.einsum('hdy,hdx->hyx', kh, q2) + f64(attn_bias)[None]
    e = np.exp(sc - sc.max(axis=1, keepdims=True))
    a = e / e.sum(axis=1, keepdims=True)
    return np.einsum('yhd,hyx->hdx', vh, a).reshape(H * D, N)

@@ -1,0 +1,134 @@
+import concourse.mybir as mybir
+from concourse.masks import make_identity
+
+P = 128
+H = 4
+N = 512
+NB = N // P
+TILES = H * NB
+AHEAD = 2
+LAG = 3
+
+FLOPS = 2 * H * P * N + 2 * 2 * H * P * N * N
+
+BF16 = mybir.dt.bfloat16
+F32 = mybir.dt.float32
+U16 = mybir.dt.uint16
+ADD = mybir.AluOpType.add
+MULT = mybir.AluOpType.mult
+EXP = mybir.ActivationFunctionType.Exp
+X = mybir.AxisListType.X
+
+
+def block(i):
+    return slice(i * P, (i + 1) * P)
+
+
+def tile_relativemultiheadattention_kernel(tc, r_emb, q, k, v, r_bias, attn_bias, offs, out):
+    nc = tc.nc
+    with tc.tile_pool(name="held", bufs=1) as held:
+        ident_bf = held.tile([P, P], BF16, name="ident_bf")
+        make_identity(nc, ident_bf[:])
+        ident_f = held.tile([P, P], F32, name="ident_f")
+        make_identity(nc, ident_f[:])
+
+        offsets = held.tile([P, N // 16], U16, name="offsets")
+        nc.sync.dma_start(offsets[:], offs)
+        rb_rows = held.tile([H, P], BF16, name="rb_rows")
+        nc.sync.dma_start(rb_rows[:], r_bias.rearrange("(h d) o -> h (d o)", h=H))
+        table = held.tile([P, N], F32, name="table")
+        nc.scalar.dma_start(table[:], r_emb)
+        q_sb = held.tile([P, H, N], BF16, name="q_sb")
+        k_sb = held.tile([P, H, N], BF16, name="k_sb")
+        for h in range(H):
+            nc.sync.dma_start(q_sb[:, h, :], q[block(h), :])
+            nc.sync.dma_start(k_sb[:, h, :], k[block(h), :])
+        bias_sb = held.tile([P, NB, N], F32, name="bias_sb")
+        bias_view = attn_bias.rearrange("(b y) j -> y b j", b=NB)
+        for jb in range(NB):
+            nc.scalar.dma_start(bias_sb[:, :, block(jb)], bias_view[:, :, block(jb)])
+        v_sb = held.tile([P, NB, H * P], BF16, name="v_sb")
+        nc.gpsimd.dma_start(v_sb[:], v.rearrange("(b y) c -> y b c", b=NB))
+
+        rb_cols = held.tile([P, H], BF16, name="rb_cols")
+        with tc.psum_pool(name="setup_psum", bufs=1) as setup_psum:
+            rb_cols_ps = setup_psum.tile([P, H], BF16, name="rb_cols_ps")
+            nc.tensor.transpose(rb_cols_ps[:], rb_rows[:], ident_bf[:H, :H])
+            nc.vector.tensor_copy(rb_cols[:], rb_cols_ps[:])
+
+        with (
+            tc.tile_pool(name="queries", bufs=AHEAD + 3) as queries,
+            tc.tile_pool(name="per_head", bufs=2) as per_head,
+            tc.tile_pool(name="work", bufs=LAG + 2) as work,
+            tc.psum_pool(name="qr_psum", bufs=1) as qr_psum,
+            tc.psum_pool(name="score_psum", bufs=4) as score_psum,
+            tc.psum_pool(name="flip_psum", bufs=2) as flip_psum,
+            tc.psum_pool(name="out_psum", bufs=1) as out_psum,
+        ):
+            qr_of_head = {}
+
+            def make_q2(h, jb):
+                if jb == 0:
+                    qr_ps = qr_psum.tile([P, N], F32, name="qr_ps")
+                    nc.tensor.matmul(qr_ps[:], lhsT=rb_cols[:, h : h + 1].to_broadcast([P, P]), rhs=q_sb[:, h, :], start=True, stop=True)
+                    qr_sb = per_head.tile([P, N], F32, name="qr_sb")
+                    nc.scalar.copy(qr_sb[:], qr_ps[:])
+                    qr_of_head[h] = qr_sb
+                piece = offsets[:, jb * (P // 16) : (jb + 1) * (P // 16)]
+                picked = queries.tile([P, P], F32, name="picked")
+                nc.vector.tensor_tensor(picked[:], table[:].indirect(piece), qr_of_head[h][:, block(jb)], MULT)
+                q2 = queries.tile([P, P], BF16, name="q2")
+                nc.gpsimd.tensor_tensor(q2[:], picked[:], q_sb[:, h, block(jb)], ADD)
+                return q2
+
+            def exponentials(h, jb, q2):
+                score = score_psum.tile([P, N], F32, name="score")
+                for yb in range(NB):
+                    nc.tensor.matmul(
+                        score[:, block(yb)],
+                        lhsT=bias_sb[:, yb, block(jb)],
+                        rhs=ident_f[:],
+                        is_transpose=True,
+                        start=(yb == 0),
+                        stop=False,
+                    )
+                nc.tensor.matmul(score[:], lhsT=q2[:], rhs=k_sb[:, h, :], start=False, stop=True)
+                neg_max = work.tile([P, 1], F32, name="neg_max")
+                nc.vector.reduce_max(neg_max[:], score[:], axis=X, negate=True)
+                expo = work.tile([P, N], F32, name="expo")
+                total = work.tile([P, 1], F32, name="total")
+                nc.scalar.activation(expo[:], score[:], EXP, bias=neg_max[:], scale=1.0, accum_out=total[:])
+                return expo, total
+
+            def apply(h, jb, expo, total):
+                inv_total = work.tile([P, 1], F32, name="inv_total")
+                nc.vector.reciprocal(inv_total[:], total[:])
+                weights = work.tile([P, N], BF16, name="weights")
+                nc.vector.tensor_scalar_mul(weights[:], expo[:], inv_total[:])
+                flipped = flip_psum.tile([P, NB, P], BF16, name="flipped")
+                for yb in range(NB):
+                    nc.tensor.matmul(flipped[:, yb, :], lhsT=weights[:, block(yb)], rhs=ident_bf[:], start=True, stop=True)
+                weights_t = work.tile([P, NB, P], BF16, name="weights_t")
+                nc.scalar.copy(weights_t[:], flipped[:])
+                out_ps = out_psum.tile([P, P], F32, name="out_ps")
+                for yb in range(NB):
+                    nc.tensor.matmul(
+                        out_ps[:],
+                        lhsT=v_sb[:, yb, block(h)],
+                        rhs=weights_t[:, yb, :],
+                        start=(yb == 0),
+                        stop=(yb == NB - 1),
+                    )
+                out_sb = work.tile([P, P], F32, name="out_sb")
+                nc.scalar.copy(out_sb[:], out_ps[:])
+                nc.sync.dma_start(out[block(h), block(jb)], out_sb[:])
+
+            q2_of_unit = {}
+            expo_of_unit = {}
+            for t in range(-AHEAD, TILES + LAG):
+                if t + AHEAD < TILES:
+                    q2_of_unit[t + AHEAD] = make_q2(*divmod(t + AHEAD, NB))
+                if 0 <= t < TILES:
+                    expo_of_unit[t] = exponentials(*divmod(t, NB), q2_of_unit.pop(t))
+                if t >= LAG:
+                    apply(*divmod(t - LAG, NB), *expo_of_unit.pop(t - LAG))

@@ -103,24 +103,35 @@ def tile_relativemultiheadattention_kernel(tc, r_emb, q, k, v, r_bias, attn_bias
             def apply(h, jb, expo, total):
                 inv_total = work.tile([P, 1], F32, name="inv_total")
                 nc.vector.reciprocal(inv_total[:], total[:])
+                drain = h * NB + jb >= TILES - LAG
                 weights = work.tile([P, N], BF16, name="weights")
-                nc.vector.tensor_scalar_mul(weights[:], expo[:], inv_total[:])
-                flipped = flip_psum.tile([P, NB, P], BF16, name="flipped")
-                for yb in range(NB):
-                    nc.tensor.matmul(flipped[:, yb, :], lhsT=weights[:, block(yb)], rhs=ident_bf[:], start=True, stop=True)
                 weights_t = work.tile([P, NB, P], BF16, name="weights_t")
-                nc.scalar.copy(weights_t[:], flipped[:])
-                out_ps = out_psum.tile([P, P], F32, name="out_ps")
-                for yb in range(NB):
-                    nc.tensor.matmul(
-                        out_ps[:],
-                        lhsT=v_sb[:, yb, block(h)],
-                        rhs=weights_t[:, yb, :],
-                        start=(yb == 0),
-                        stop=(yb == NB - 1),
-                    )
+                if drain:
+                    out_ps = score_psum.tile([P, N], F32, name="out_ps_in_drain", tag="score")[:, :P]
+                else:
+                    out_ps = out_psum.tile([P, P], F32, name="out_ps")[:]
+                pieces = 2 if h * NB + jb == TILES - 1 else 1
+                for piece in range(pieces):
+                    first, end = piece * NB // pieces, (piece + 1) * NB // pieces
+                    keys = slice(first * P, end * P)
+                    nc.vector.tensor_scalar_mul(weights[:, keys], expo[:, keys], inv_total[:])
+                    flipped = flip_psum.tile([P, NB, P], BF16, name="flipped")
+                    for yb in range(first, end):
+                        nc.tensor.matmul(flipped[:, yb, :], lhsT=weights[:, block(yb)], rhs=ident_bf[:], start=True, stop=True)
+                    if drain and piece == 0:
+                        nc.vector.tensor_copy(weights_t[:, first:end, :], flipped[:, first:end, :])
+                    else:
+                        nc.scalar.copy(weights_t[:, first:end, :], flipped[:, first:end, :])
+                    for yb in range(first, end):
+                        nc.tensor.matmul(
+                            out_ps,
+                            lhsT=v_sb[:, yb, block(h)],
+                            rhs=weights_t[:, yb, :],
+                            start=(yb == 0),
+                            stop=(yb == NB - 1),
+                        )
                 out_sb = work.tile([P, P], F32, name="out_sb")
-                nc.scalar.copy(out_sb[:], out_ps[:])
+                nc.scalar.copy(out_sb[:], out_ps)
                 nc.sync.dma_start(out[block(h), block(jb)], out_sb[:])
 
             q2_of_unit = {}

import concourse.mybir as mybir
from concourse.masks import make_identity

P = 128
H = 4
N = 512
NB = N // P
TILES = H * NB
AHEAD = 2
LAG = 3

FLOPS = 2 * H * P * N + 2 * 2 * H * P * N * N

BF16 = mybir.dt.bfloat16
F32 = mybir.dt.float32
U16 = mybir.dt.uint16
ADD = mybir.AluOpType.add
MULT = mybir.AluOpType.mult
EXP = mybir.ActivationFunctionType.Exp
X = mybir.AxisListType.X


def block(i):
    return slice(i * P, (i + 1) * P)


def tile_relativemultiheadattention_kernel(tc, r_emb, q, k, v, r_bias, attn_bias, offs, out):
    nc = tc.nc
    with tc.tile_pool(name="held", bufs=1) as held:
        ident_bf = held.tile([P, P], BF16, name="ident_bf")
        make_identity(nc, ident_bf[:])
        ident_f = held.tile([P, P], F32, name="ident_f")
        make_identity(nc, ident_f[:])

        offsets = held.tile([P, N // 16], U16, name="offsets")
        nc.sync.dma_start(offsets[:], offs)
        rb_rows = held.tile([H, P], BF16, name="rb_rows")
        nc.sync.dma_start(rb_rows[:], r_bias.rearrange("(h d) o -> h (d o)", h=H))
        table = held.tile([P, N], F32, name="table")
        nc.scalar.dma_start(table[:], r_emb)
        q_sb = held.tile([P, H, N], BF16, name="q_sb")
        k_sb = held.tile([P, H, N], BF16, name="k_sb")
        for h in range(H):
            nc.sync.dma_start(q_sb[:, h, :], q[block(h), :])
            nc.sync.dma_start(k_sb[:, h, :], k[block(h), :])
        bias_sb = held.tile([P, NB, N], F32, name="bias_sb")
        bias_view = attn_bias.rearrange("(b y) j -> y b j", b=NB)
        for jb in range(NB):
            nc.scalar.dma_start(bias_sb[:, :, block(jb)], bias_view[:, :, block(jb)])
        v_sb = held.tile([P, NB, H * P], BF16, name="v_sb")
        nc.gpsimd.dma_start(v_sb[:], v.rearrange("(b y) c -> y b c", b=NB))

        rb_cols = held.tile([P, H], BF16, name="rb_cols")
        with tc.psum_pool(name="setup_psum", bufs=1) as setup_psum:
            rb_cols_ps = setup_psum.tile([P, H], BF16, name="rb_cols_ps")
            nc.tensor.transpose(rb_cols_ps[:], rb_rows[:], ident_bf[:H, :H])
            nc.vector.tensor_copy(rb_cols[:], rb_cols_ps[:])

        with (
            tc.tile_pool(name="queries", bufs=AHEAD + 3) as queries,
            tc.tile_pool(name="per_head", bufs=2) as per_head,
            tc.tile_pool(name="work", bufs=LAG + 2) as work,
            tc.psum_pool(name="qr_psum", bufs=1) as qr_psum,
            tc.psum_pool(name="score_psum", bufs=4) as score_psum,
            tc.psum_pool(name="flip_psum", bufs=2) as flip_psum,
            tc.psum_pool(name="out_psum", bufs=1) as out_psum,
        ):
            qr_of_head = {}

            def make_q2(h, jb):
                if jb == 0:
                    qr_ps = qr_psum.tile([P, N], F32, name="qr_ps")
                    nc.tensor.matmul(qr_ps[:], lhsT=rb_cols[:, h : h + 1].to_broadcast([P, P]), rhs=q_sb[:, h, :], start=True, stop=True)
                    qr_sb = per_head.tile([P, N], F32, name="qr_sb")
                    nc.scalar.copy(qr_sb[:], qr_ps[:])
                    qr_of_head[h] = qr_sb
                piece = offsets[:, jb * (P // 16) : (jb + 1) * (P // 16)]
                picked = queries.tile([P, P], F32, name="picked")
                nc.vector.tensor_tensor(picked[:], table[:].indirect(piece), qr_of_head[h][:, block(jb)], MULT)
                q2 = queries.tile([P, P], BF16, name="q2")
                nc.gpsimd.tensor_tensor(q2[:], picked[:], q_sb[:, h, block(jb)], ADD)
                return q2

            def exponentials(h, jb, q2):
                score = score_psum.tile([P, N], F32, name="score")
                for yb in range(NB):
                    nc.tensor.matmul(
                        score[:, block(yb)],
                        lhsT=bias_sb[:, yb, block(jb)],
                        rhs=ident_f[:],
                        is_transpose=True,
                        start=(yb == 0),
                        stop=False,
                    )
                nc.tensor.matmul(score[:], lhsT=q2[:], rhs=k_sb[:, h, :], start=False, stop=True)
                neg_max = work.tile([P, 1], F32, name="neg_max")
                nc.vector.reduce_max(neg_max[:], score[:], axis=X, negate=True)
                expo = work.tile([P, N], F32, name="expo")
                total = work.tile([P, 1], F32, name="total")
                nc.scalar.activation(expo[:], score[:], EXP, bias=neg_max[:], scale=1.0, accum_out=total[:])
                return expo, total

            def apply(h, jb, expo, total):
                inv_total = work.tile([P, 1], F32, name="inv_total")
                nc.vector.reciprocal(inv_total[:], total[:])
                drain = h * NB + jb >= TILES - LAG
                weights = work.tile([P, N], BF16, name="weights")
                weights_t = work.tile([P, NB, P], BF16, name="weights_t")
                if drain:
                    out_ps = score_psum.tile([P, N], F32, name="out_ps_in_drain", tag="score")[:, :P]
                else:
                    out_ps = out_psum.tile([P, P], F32, name="out_ps")[:]
                pieces = 2 if h * NB + jb == TILES - 1 else 1
                for piece in range(pieces):
                    first, end = piece * NB // pieces, (piece + 1) * NB // pieces
                    keys = slice(first * P, end * P)
                    nc.vector.tensor_scalar_mul(weights[:, keys], expo[:, keys], inv_total[:])
                    flipped = flip_psum.tile([P, NB, P], BF16, name="flipped")
                    for yb in range(first, end):
                        nc.tensor.matmul(flipped[:, yb, :], lhsT=weights[:, block(yb)], rhs=ident_bf[:], start=True, stop=True)
                    if drain and piece == 0:
                        nc.vector.tensor_copy(weights_t[:, first:end, :], flipped[:, first:end, :])
                    else:
                        nc.scalar.copy(weights_t[:, first:end, :], flipped[:, first:end, :])
                    for yb in range(first, end):
                        nc.tensor.matmul(
                            out_ps,
                            lhsT=v_sb[:, yb, block(h)],
                            rhs=weights_t[:, yb, :],
                            start=(yb == 0),
                            stop=(yb == NB - 1),
                        )
                out_sb = work.tile([P, P], F32, name="out_sb")
                nc.scalar.copy(out_sb[:], out_ps)
                nc.sync.dma_start(out[block(h), block(jb)], out_sb[:])

            q2_of_unit = {}
            expo_of_unit = {}
            for t in range(-AHEAD, TILES + LAG):
                if t + AHEAD < TILES:
                    q2_of_unit[t + AHEAD] = make_q2(*divmod(t + AHEAD, NB))
                if 0 <= t < TILES:
                    expo_of_unit[t] = exponentials(*divmod(t, NB), q2_of_unit.pop(t))
                if t >= LAG:
                    apply(*divmod(t - LAG, NB), *expo_of_unit.pop(t - LAG))
